import numpy as np
import ml_dtypes


def mxq(x, axis, fmt="e4m3"):
    dtype, down = {"e4m3": (ml_dtypes.float8_e4m3fn, 7), "e5m2": (ml_dtypes.float8_e5m2, 14)}[fmt]
    v = np.moveaxis(np.asarray(x, np.float32).astype(ml_dtypes.bfloat16).astype(np.float64), axis, -1)
    blocks = v.reshape(v.shape[:-1] + (-1, 32))
    amax = np.abs(blocks).max(-1, keepdims=True)
    byte = np.maximum(np.where(amax > 0, np.frexp(amax)[1] - 1 + 127, 0) - down, 1)
    scale = np.exp2(byte - 127.0)
    codes = (blocks / scale).astype(np.float32).astype(dtype).astype(np.float64)
    return np.moveaxis((codes * scale).reshape(v.shape), -1, axis)


WIDE = False


def mx_kscale(k):
    if not WIDE:
        return np.ones(k)
    levels = np.array([10, -10, 5, -5, 0])
    if k % 512:
        return np.exp2(np.random.permutation(np.resize(levels, k // 32))).repeat(32)
    a = np.empty((k // 512, 16))
    for p in range(k // 512):
        a[p, :8] = np.random.permutation(np.resize(levels, 8))
        for g in range(8):
            far = levels[np.abs(levels - a[p, g]) >= 10]
            a[p, g + 8] = far[np.random.randint(len(far))]
    return np.exp2(a.ravel()).repeat(32)


BF16 = ml_dtypes.bfloat16


def bf(x):
    return np.asarray(x, np.float32).astype(BF16)


def f64(x):
    return np.asarray(x).astype(np.float64)


E2M1 = np.array([0.0, 0.5, 1.0, 1.5, 2.0, 3.0, 4.0, 6.0, -0.0, -0.5, -1.0, -1.5, -2.0, -3.0, -4.0, -6.0])


def pack_weight(w, fmt):
    k, n = w.shape
    w = f64(bf(w)).reshape(k // 32, 32, n)
    amax = np.abs(w).max(1)
    if fmt == "e4m3":
        byte = np.frexp(amax)[1] - 1 + 127 - 7
    else:
        mant, ex = np.frexp(amax / 6.0)
        byte = np.where(mant > 0.5, ex, ex - 1) + 127
    byte = np.clip(np.where(amax > 0, byte, 1), 1, 254)
    scaled = (w * np.exp2(127.0 - byte)[:, None, :]).reshape(k, n).astype(np.float32)
    by_word = np.ascontiguousarray(scaled.reshape(k // 512, 128, 4, n).transpose(0, 1, 3, 2))
    if fmt == "e4m3":
        words = by_word.astype(ml_dtypes.float8_e4m3fn).view(np.uint8)
    else:
        c = by_word.astype(ml_dtypes.float4_e2m1fn).view(np.uint8) & 0xF
        words = c[..., 0::2] | (c[..., 1::2] << 4)
    return np.ascontiguousarray(words), np.ascontiguousarray(byte.astype(np.uint8).reshape(k // 512, 16, n))


def unpack_weight(words, scales, fmt):
    g, p, n, _ = words.shape
    if fmt == "e4m3":
        vals = np.ascontiguousarray(words).view(ml_dtypes.float8_e4m3fn).astype(np.float64)
    else:
        nib = np.empty((g, p, n, 4), np.uint8)
        nib[..., 0::2] = words & 0xF
        nib[..., 1::2] = words >> 4
        vals = E2M1[nib]
    vals = vals * np.repeat(np.exp2(scales.astype(np.float64) - 127.0), 8, axis=1)[..., None]
    return vals.transpose(0, 1, 3, 2).reshape(g * 512, n)
def pack4(w):
    words, scales = pack_weight(w, "e2m1")
    return words.reshape(words.shape[0], 128, -1), scales


def unpack4(words, scales):
    return unpack_weight(words.reshape(words.shape[0], 128, -1, 2), scales, "e2m1")


B, S, D, H, HD, M, G = 4, 128, 1024, 8, 128, 4096, 3
EPS = 1e-6
HH = H * HD


def silu(v):
    return v / (1.0 + np.exp(-v))


def rmsnorm(x, gain):
    var = np.mean(np.square(x), axis=-1, keepdims=True)
    return x * (1.0 / np.sqrt(var + EPS)) * gain


def draw0():
    s, t = mx_kscale(HH), mx_kscale(D)
    attn = bf(0.3 * np.random.standard_normal((B, S, HH)) * s)
    x = bf(np.random.standard_normal((B, S, D)))
    w_o_words, w_o_scales = pack4(np.random.standard_normal((HH, D)) * 2.0 / np.sqrt(HH) / s[:, None])
    rms2_scale = bf((1.0 + 0.1 * np.random.standard_normal(D)) * t)
    w_gate_words, w_gate_scales = pack4(np.random.standard_normal((D, M)) / np.sqrt(D) / t[:, None])
    w_up_words, w_up_scales = pack4(np.random.standard_normal((D, M)) / np.sqrt(D) / t[:, None])
    return {"attn": attn,
            "x": x,
            "w_o_words": w_o_words,
            "w_o_scales": w_o_scales,
            "rms2_scale": rms2_scale,
            "w_gate_words": w_gate_words,
            "w_gate_scales": w_gate_scales,
            "w_up_words": w_up_words,
            "w_up_scales": w_up_scales}


def core(attn, x, w_o_words, w_o_scales, rms2_scale, w_gate_words, w_gate_scales, w_up_words, w_up_scales):
    x_mid = f64(x) + (mxq(f64(attn), 2, "e4m3") @ unpack4(w_o_words, w_o_scales))
    hq = mxq(rmsnorm(x_mid, f64(rms2_scale)), 2, "e4m3")
    g = silu(hq @ unpack4(w_gate_words, w_gate_scales)) * (hq @ unpack4(w_up_words, w_up_scales))
    return x_mid, g


def e4m3fn_bytes(y):
    return np.clip(np.asarray(y, np.float64), -448.0, 448.0).astype(np.float32).astype(ml_dtypes.float8_e4m3fn).view(np.uint8)


def e4m3fn_values(b):
    return np.asarray(b, np.uint8).view(ml_dtypes.float8_e4m3fn).astype(np.float64)


def setup_inputs():
    d = draw0()
    x0 = np.asarray(d['attn']).astype(np.float64)
    s = (np.max(np.abs(x0), axis=(0, 1), keepdims=True) / 448.0).astype(np.float32)
    out = {}
    for k, v in d.items():
        if k == 'attn':
            out['attn_bytes'] = e4m3fn_bytes(x0 / s.astype(np.float64))
            out['attn_scale'] = s
        else:
            out[k] = v
    return out


def reference(attn_bytes, attn_scale, x, w_o_words, w_o_scales, rms2_scale, w_gate_words, w_gate_scales, w_up_words, w_up_scales):
    return core(e4m3fn_values(attn_bytes) * attn_scale.astype(np.float64), x, w_o_words, w_o_scales, rms2_scale, w_gate_words, w_gate_scales, w_up_words, w_up_scales)

@@ -1,0 +1,354 @@
+from contextlib import ExitStack
+
+import concourse.mybir as mybir
+from concourse.masks import make_identity
+
+F32 = mybir.dt.float32
+BF16 = mybir.dt.bfloat16
+I32 = mybir.dt.int32
+U32 = mybir.dt.uint32
+U8 = mybir.dt.uint8
+F8 = mybir.dt.float8_e4m3fn
+FP8X4 = mybir.dt.float8_e4m3fn_x4
+FP4X4 = mybir.dt.float4_e2m1fn_x4
+ACT = mybir.ActivationFunctionType
+ALU = mybir.AluOpType
+
+P = 128
+D = 1024
+M = 4096
+NT = 4
+EPS = 1e-6
+NC = 512
+CHUNKS = M // NC
+
+FLOPS = 2 * NT * P * D * (D + 2 * M)
+
+
+def tile_transformerblocktpu_pb_w4_kernel(
+    tc, attn_bytes, attn_scale, x, w_o_words, w_o_scales, rms2_scale,
+    w_gate_words, w_gate_scales, w_up_words, w_up_scales, out_0, out_1,
+):
+    nc = tc.nc
+    with ExitStack() as ctx:
+        keep = ctx.enter_context(tc.tile_pool(name="keep", bufs=1))
+        work = ctx.enter_context(tc.tile_pool(name="work", bufs=4))
+        outp = ctx.enter_context(tc.tile_pool(name="outp", bufs=6))
+        psum = ctx.enter_context(tc.psum_pool(name="psum", bufs=1))
+        ctx.enter_context(tc.manual_schedule())
+
+        count = [0]
+
+        def bank(shape):
+            k = count[0] % 8
+            count[0] += 1
+            b = psum.tile(shape, F32, name="bank" + str(k), tag="bank" + str(k))
+            return b
+
+        a_bytes = keep.tile([P, NT, D], U8, align_bytes=64, name="a_bytes")
+        a_sc = keep.tile([P, 2, 4], F32, align_bytes=64, name="a_sc")
+        x_sb = keep.tile([P, NT, D], BF16, align_bytes=64, name="x_sb")
+        wo = keep.tile([P, 2, 2 * D], U8, align_bytes=64, name="wo")
+        wo_sc = keep.tile([P, 2, D], U8, align_bytes=64, name="wo_sc")
+        wg_sc = keep.tile([P, 2, M], U8, align_bytes=64, name="wg_sc")
+        wu_sc = keep.tile([P, 2, M], U8, align_bytes=64, name="wu_sc")
+        ident = keep.tile([P, P], F32, align_bytes=64, name="ident")
+        ones = keep.tile([P, P], BF16, align_bytes=64, name="ones")
+        gain_row = keep.tile([P, D], BF16, align_bytes=64, name="gain_row")
+        gain = keep.tile([P, D], BF16, align_bytes=64, name="gain")
+        neghalf = keep.tile([P, 1], F32, align_bytes=64, name="neghalf")
+        warm = keep.tile([P, 2], F32, align_bytes=64, name="warm")
+        xmid = []
+        for i in range(NT):
+            t = keep.tile([P, D], F32, align_bytes=64, name="xmid" + str(i))
+            xmid.append(t)
+        sqj = keep.tile([P, NC], F32, align_bytes=64, name="sqj")
+
+        nc.gpsimd.memset(warm[:, 0:1], 0.0)
+        nc.gpsimd.memset(ones[:], 1.0)
+        nc.scalar.activation(out=warm[:, 1:2], in_=warm[:, 0:1], func=ACT.Silu)
+        nc.vector.memset(gain_row[:], 0.0)
+        nc.vector.memset(wo_sc[:].rearrange("p g n -> p (g n)").bitcast(I32), 0)
+        nc.vector.memset(wg_sc[:].rearrange("p g n -> p (g n)").bitcast(I32), 0)
+
+        nc.sync.dma_start(out=a_bytes[:, 0, :], in_=attn_bytes[0])
+        nc.scalar.dma_start(out=a_sc[:], in_=attn_scale.rearrange("a b (g p t) -> p (a b g) t", p=P, t=4))
+        make_identity(nc, ident[:])
+        nc.gpsimd.memset(wu_sc[:].rearrange("p g n -> p (g n)").bitcast(I32), 0)
+        nc.gpsimd.memset(neghalf[:], -0.5)
+        nc.scalar.dma_start(out=gain_row[0:1, :], in_=rms2_scale.unsqueeze(0))
+
+        def load_scales(dst, src):
+            for q in range(4):
+                nc.sync.dma_start(
+                    out=dst[32 * q : 32 * q + 4, :, :].bitcast(I32),
+                    in_=src[:, 4 * q : 4 * q + 4, :].rearrange("g q n -> q g n").bitcast(I32),
+                )
+
+        def load_words(dst, src, lo, hi):
+            nc.sync.dma_start(out=dst[:], in_=src[:, :, 2 * lo : 2 * hi].rearrange("g p b -> p g b"))
+
+        load_scales(wo_sc, w_o_scales)
+        load_words(wo, w_o_words, 0, D)
+        nc.scalar.dma_start(out=x_sb[:, 0, :], in_=x[0])
+        nc.sync.dma_start(out=a_bytes[:, 1, :], in_=attn_bytes[1])
+        load_scales(wg_sc, w_gate_scales)
+        load_scales(wu_sc, w_up_scales)
+        wg = {}
+        wu = {}
+        for lo, hi in ((0, 512), (512, 1024), (1024, 2048), (2048, 3072), (3072, 4096)):
+            tg = keep.tile([P, 2, 2 * (hi - lo)], U8, align_bytes=64, name="wg" + str(lo))
+            tu = keep.tile([P, 2, 2 * (hi - lo)], U8, align_bytes=64, name="wu" + str(lo))
+            load_words(tg, w_gate_words, lo, hi)
+            load_words(tu, w_up_words, lo, hi)
+            for c in range(lo // NC, hi // NC):
+                wg[c] = (tg, 2 * (NC * c - lo))
+                wu[c] = (tu, 2 * (NC * c - lo))
+            if lo == 512:
+                nc.sync.dma_start(out=x_sb[:, 1, :], in_=x[1])
+            if lo == 1024:
+                nc.sync.dma_start(out=a_bytes[:, 2:NT, :], in_=attn_bytes[2:NT].rearrange("i p d -> p i d"))
+        nc.sync.dma_start(out=x_sb[:, 2, :], in_=x[2])
+        nc.sync.dma_start(out=x_sb[:, 3, :], in_=x[3])
+
+        abf = {}
+        tbank = {}
+        agrp = {}
+        acod = {}
+        asca = {}
+        pbank = {}
+        ss = {}
+        rstd = {}
+        hbf = {}
+        hbank = {}
+        hgrp = {}
+        hcod = {}
+        hsca = {}
+
+        def cast(i, g, on_vector):
+            if i not in abf:
+                t = work.tile([P, D], BF16, align_bytes=64, name="abf")
+                abf[i] = t
+            o = abf[i][:, NC * g : NC * (g + 1)]
+            s = a_bytes[:, i, NC * g : NC * (g + 1)].bitcast(F8)
+            if on_vector:
+                nc.vector.tensor_copy(out=o, in_=s)
+            else:
+                nc.scalar.copy(out=o, in_=s)
+
+        def turn_attn(i, g):
+            if i > 1 and g == 1:
+                tbank[(i, 1)] = tbank[(i, 0)][:, 1]
+            else:
+                b = bank([P, 2, 2, P])
+                tbank[(i, g)] = b[:, 0] if i <= 1 else b
+            dst = tbank[(i, g)] if i <= 1 or g == 1 else tbank[(i, g)][:, 0]
+            words = abf[i][:].bitcast(F32)
+            for u in (0, 1):
+                nc.tensor.transpose(dst[:, u, :], words[:, 256 * g + u : 256 * (g + 1) : 2], ident[:])
+
+        def scale_attn(i, g):
+            if i not in agrp:
+                t = work.tile([P, 2, P, 2, 2], BF16, align_bytes=64, name="agrp")
+                agrp[i] = t
+            src = tbank[(i, g)] if i <= 1 or g == 1 else tbank[(i, g)][:, 0]
+            src = src.rearrange("p u r -> p (u r)").bitcast(BF16)
+            src = src.rearrange("p (u r e) -> p r u e", u=2, e=2)
+            sc = a_sc[:, g, :].rearrange("p (u e) -> p u e", u=2).unsqueeze(1).to_broadcast([P, P, 2, 2])
+            nc.vector.tensor_tensor(out=agrp[i][:, g], in0=src, in1=sc, op=ALU.mult)
+
+        def quant_attn(i, lo, hi):
+            if i not in acod:
+                t = work.tile([P, 2 * P], U32, align_bytes=64, name="acod")
+                acod[i] = t
+                t2 = work.tile([P, 2 * P], U8, align_bytes=64, name="asca")
+                asca[i] = t2
+            nc.vector.quantize_mx(
+                out=acod[i][:, P * lo : P * hi].bitcast(FP8X4),
+                scales=asca[i][:, P * lo : P * hi],
+                in_=agrp[i][:, lo:hi].rearrange("p g r u e -> p (g r u e)"),
+            )
+
+        def mm1(i):
+            pbank[i] = [bank([P, NC]), bank([P, NC])]
+            for n in (0, 1):
+                for g in (0, 1):
+                    nc.tensor.matmul_mx(
+                        out=pbank[i][n][:],
+                        lhsT=acod[i][:, P * g : P * (g + 1)].bitcast(FP8X4),
+                        lhsT_scale=asca[i][:, P * g : P * (g + 1)],
+                        rhs=wo[:, g, 2 * NC * n : 2 * NC * (n + 1)].bitcast(FP4X4),
+                        rhs_scale=wo_sc[:, g, NC * n : NC * (n + 1)],
+                        start=(g == 0),
+                        stop=(g == 1),
+                    )
+
+        def add_x(i, n):
+            cols = slice(NC * n, NC * (n + 1))
+            nc.vector.tensor_tensor(out=xmid[i][:, cols], in0=pbank[i][n][:], in1=x_sb[:, i, cols], op=ALU.add)
+
+        def square(i, n):
+            if i not in ss:
+                t = work.tile([P, 2], F32, align_bytes=64, name="ss")
+                ss[i] = t
+            cols = slice(NC * n, NC * (n + 1))
+            nc.scalar.activation(out=sqj[:], in_=xmid[i][:, cols], func=ACT.Square, scale=1.0 / 32.0, accum_out=ss[i][:, n : n + 1])
+
+        def root(i):
+            ms = work.tile([P, 1], F32, align_bytes=64, name="ms")
+            r = work.tile([P, 1], F32, align_bytes=64, name="rstd")
+            nc.gpsimd.tensor_scalar(out=ms[:], in0=ss[i][:, 0:1], scalar1=ss[i][:, 1:2], scalar2=EPS, op0=ALU.add, op1=ALU.add)
+            nc.gpsimd.tensor_tensor(out=r[:], in0=ms[:], in1=neghalf[:], op=ALU.pow)
+            rstd[i] = r
+
+        def split_words(ap):
+            return ap.rearrange("q (p u e) -> q u p e", u=2, e=2)
+
+        def h_tile(i):
+            if i not in hbf:
+                t = work.tile([P, 2, 2, P, 2], BF16, align_bytes=64, name="hbf")
+                hbf[i] = t
+
+        ys = {}
+
+        def gain_y(i, g, engine):
+            if i not in ys:
+                t = work.tile([P, 2, NC], F32, align_bytes=64, name="y", bufs=2)
+                ys[i] = t
+            cols = slice(NC * g, NC * (g + 1))
+            engine.tensor_tensor(
+                out=ys[i][:, g].rearrange("q (u p e) -> q u p e", u=2, e=2),
+                in0=split_words(xmid[i][:, cols]), in1=split_words(gain[:, cols]), op=ALU.mult)
+
+        def h_norm(i, lo, hi):
+            h_tile(i)
+            nc.vector.tensor_scalar(
+                out=hbf[i][:, lo:hi].rearrange("q g u p e -> q (g u p e)"),
+                in0=ys[i][:, lo:hi].rearrange("q g k -> q (g k)"), scalar1=rstd[i][:], scalar2=None, op0=ALU.mult)
+
+        def turn_h(i, g):
+            b = bank([P, 2, P])
+            hbank[(i, g)] = b
+            words = hbf[i][:].rearrange("q g u p e -> q (g u p e)").bitcast(F32)
+            for u in (0, 1):
+                nc.tensor.transpose(b[:, u, :], words[:, P * (2 * g + u) : P * (2 * g + u + 1)], ident[:])
+
+        def copy_h(i, g, on_vector):
+            if i not in hgrp:
+                t = work.tile([P, 2, 4 * P], BF16, align_bytes=64, name="hgrp")
+                hgrp[i] = t
+            o = hgrp[i][:, g].bitcast(F32).rearrange("p (r u) -> p r u", u=2)
+            s = hbank[(i, g)][:].rearrange("p u r -> p r u")
+            if on_vector:
+                nc.vector.tensor_copy(out=o, in_=s)
+            else:
+                nc.scalar.copy(out=o, in_=s)
+
+        def quant_h(i):
+            t = work.tile([P, 2 * P], U32, align_bytes=64, name="hcod")
+            t2 = work.tile([P, 2 * P], U8, align_bytes=64, name="hsca")
+            hcod[i], hsca[i] = t, t2
+            nc.vector.quantize_mx(out=t[:].bitcast(FP8X4), scales=t2[:], in_=hgrp[i][:].rearrange("p g w -> p (g w)"))
+
+        def mm2(i, c, w, w_sc, lo, width):
+            b = bank([P, width])
+            step = NC if width == NC else P
+            for at_col in range(0, width, step):
+              for g in (0, 1):
+                nc.tensor.matmul_mx(
+                    out=b[:, at_col : at_col + step],
+                    lhsT=hcod[i][:, P * g : P * (g + 1)].bitcast(FP8X4),
+                    lhsT_scale=hsca[i][:, P * g : P * (g + 1)],
+                    rhs=w[c][0][:, g, w[c][1] + 2 * (lo + at_col) : w[c][1] + 2 * (lo + at_col + step)].bitcast(FP4X4),
+                    rhs_scale=w_sc[:, g, NC * c + lo + at_col : NC * c + lo + at_col + step],
+                    start=(g == 0),
+                    stop=(g == 1),
+                )
+            return b
+
+        def store_xmid(i):
+            nc.sync.dma_start(out=out_0[i], in_=xmid[i][:])
+
+        def dummies(k):
+            b = bank([P, NC])
+            for j in range(k):
+                nc.tensor.matmul(b[:, :P], ones[:], ones[:], start=True, stop=True)
+
+        dummies(10)
+        cast(0, 0, True)
+        cast(0, 1, False)
+        turn_attn(0, 0)
+        turn_attn(0, 1)
+        gb = [bank([P, NC]), bank([P, NC])]
+        for n in (0, 1):
+            nc.tensor.matmul(gb[n][:], ones[:], gain_row[:, NC * n : NC * (n + 1)], start=True, stop=True)
+        for n in (0, 1):
+            nc.scalar.copy(out=gain[:, NC * n : NC * (n + 1)], in_=gb[n][:])
+        scale_attn(0, 0)
+        scale_attn(0, 1)
+        quant_attn(0, 0, 1)
+        quant_attn(0, 1, 2)
+        mm1(0)
+        cast(1, 0, False)
+        cast(1, 1, False)
+        add_x(0, 0)
+        square(0, 0)
+        add_x(0, 1)
+        square(0, 1)
+        root(0)
+        turn_attn(1, 0)
+        turn_attn(1, 1)
+        gain_y(0, 0, nc.vector)
+        gain_y(0, 1, nc.vector)
+        h_norm(0, 0, 1)
+        h_norm(0, 1, 2)
+        turn_h(0, 0)
+        turn_h(0, 1)
+        scale_attn(1, 0)
+        copy_h(0, 0, False)
+        copy_h(0, 1, True)
+        dummies(8)
+        quant_h(0)
+        scale_attn(1, 1)
+        quant_attn(1, 0, 2)
+
+        at = {}
+
+        def put(pos, *fs):
+            at.setdefault(pos, []).extend(fs)
+
+        def plan_attn(i, pos):
+            put(pos, lambda: cast(i, 0, False), lambda: cast(i, 1, False))
+            put(pos + 1, lambda: (turn_attn(i, 0), turn_attn(i, 1)), lambda: scale_attn(i, 0))
+            put(pos + 2, lambda: scale_attn(i, 1), lambda: quant_attn(i, 0, 2))
+
+        def plan_rest(i, pos):
+            put(pos, lambda: mm1(i), lambda: add_x(i, 0))
+            put(pos + 1, lambda: add_x(i, 1), lambda: square(i, 0), lambda: gain_y(i, 0, nc.gpsimd))
+            put(pos + 2, lambda: square(i, 1), lambda: gain_y(i, 1, nc.gpsimd), lambda: root(i), lambda: store_xmid(i))
+            put(pos + 4, lambda: h_norm(i, 0, 2))
+            put(pos + 6, lambda: (turn_h(i, 0), turn_h(i, 1), copy_h(i, 0, False), copy_h(i, 1, False)), lambda: quant_h(i))
+
+        plan_rest(1, 0)
+        plan_attn(2, 3)
+        plan_rest(2, 7)
+        plan_attn(3, 10)
+        plan_rest(3, 15)
+
+        for i in range(NT):
+            for c in range(CHUNKS):
+                last = i == NT - 1 and c == CHUNKS - 1
+                width = NC // 2 if last else NC
+                for lo in range(0, NC, width):
+                    bg = mm2(i, c, wg, wg_sc, lo, width)
+                    bu = mm2(i, c, wu, wu_sc, lo, width)
+                    s = work.tile([P, NC], F32, align_bytes=64, name="s")
+                    nc.scalar.activation(out=s[:, :width], in_=bg[:], func=ACT.Silu)
+                    o = outp.tile([P, NC], F32, align_bytes=64, name="o")
+                    nc.vector.tensor_tensor(out=o[:, :width], in0=bu[:], in1=s[:, :width], op=ALU.mult)
+                    first = NC * c + lo
+                    nc.sync.dma_start(out=out_1[i, :, first : first + width], in_=o[:, :width])
+                if i == 0 and c == 0:
+                    store_xmid(0)
+                for step in at.get(CHUNKS * i + c, []):
+                    step()

@@ -21,6 +21,7 @@ NT = 4
 EPS = 1e-6
 NC = 512
 CHUNKS = M // NC
+SPLIT = 5 * NC
 
 FLOPS = 2 * NT * P * D * (D + 2 * M)
 
@@ -33,25 +34,27 @@ def tile_transformerblocktpu_pb_w4_kernel(
     with ExitStack() as ctx:
         keep = ctx.enter_context(tc.tile_pool(name="keep", bufs=1))
         work = ctx.enter_context(tc.tile_pool(name="work", bufs=4))
-        outp = ctx.enter_context(tc.tile_pool(name="outp", bufs=6))
+        outp = ctx.enter_context(tc.tile_pool(name="outp", bufs=10))
         psum = ctx.enter_context(tc.psum_pool(name="psum", bufs=1))
         ctx.enter_context(tc.manual_schedule())
 
+        order = [0, 1, 2, 3, 5, 0, 1, 2, 3, 4, 5]
         count = [0]
 
-        def bank(shape):
-            k = count[0] % 8
-            count[0] += 1
+        def bank(shape, k):
             b = psum.tile(shape, F32, name="bank" + str(k), tag="bank" + str(k))
             return b
+
+        def next_bank(shape):
+            n = count[0]
+            count[0] += 1
+            return bank(shape, order[n] if n < len(order) else (n - len(order)) % 6)
 
         a_bytes = keep.tile([P, NT, D], U8, align_bytes=64, name="a_bytes")
         a_sc = keep.tile([P, 2, 4], F32, align_bytes=64, name="a_sc")
         x_sb = keep.tile([P, NT, D], BF16, align_bytes=64, name="x_sb")
         wo = keep.tile([P, 2, 2 * D], U8, align_bytes=64, name="wo")
         wo_sc = keep.tile([P, 2, D], U8, align_bytes=64, name="wo_sc")
-        wg_sc = keep.tile([P, 2, M], U8, align_bytes=64, name="wg_sc")
-        wu_sc = keep.tile([P, 2, M], U8, align_bytes=64, name="wu_sc")
         ident = keep.tile([P, P], F32, align_bytes=64, name="ident")
         ones = keep.tile([P, P], BF16, align_bytes=64, name="ones")
         gain_row = keep.tile([P, D], BF16, align_bytes=64, name="gain_row")
@@ -66,37 +69,48 @@ def tile_transformerblocktpu_pb_w4_kernel(
 
         nc.gpsimd.memset(warm[:, 0:1], 0.0)
         nc.gpsimd.memset(ones[:], 1.0)
-        nc.scalar.activation(out=warm[:, 1:2], in_=warm[:, 0:1], func=ACT.Silu)
-        nc.vector.memset(gain_row[:], 0.0)
+        nc.vector.memset(gain_row[:].bitcast(I32), 0)
         nc.vector.memset(wo_sc[:].rearrange("p g n -> p (g n)").bitcast(I32), 0)
-        nc.vector.memset(wg_sc[:].rearrange("p g n -> p (g n)").bitcast(I32), 0)
+        wg_sc = []
+        wu_sc = []
+        for half, width in ((0, SPLIT), (1, M - SPLIT)):
+            t = keep.tile([P, 2, width], U8, align_bytes=64, name="wg_sc" + str(half))
+            wg_sc.append(t)
+            t2 = keep.tile([P, 2, width], U8, align_bytes=64, name="wu_sc" + str(half))
+            wu_sc.append(t2)
+
+        def clear(t):
+            nc.vector.memset(t[:].rearrange("p g n -> p (g n)").bitcast(I32), 0)
+
+        clear(wg_sc[0])
+        clear(wu_sc[0])
 
         nc.sync.dma_start(out=a_bytes[:, 0, :], in_=attn_bytes[0])
         nc.scalar.dma_start(out=a_sc[:], in_=attn_scale.rearrange("a b (g p t) -> p (a b g) t", p=P, t=4))
-        make_identity(nc, ident[:])
-        nc.gpsimd.memset(wu_sc[:].rearrange("p g n -> p (g n)").bitcast(I32), 0)
-        nc.gpsimd.memset(neghalf[:], -0.5)
         nc.scalar.dma_start(out=gain_row[0:1, :], in_=rms2_scale.unsqueeze(0))
+        nc.scalar.activation(out=warm[:, 1:2], in_=warm[:, 0:1], func=ACT.Silu)
+        make_identity(nc, ident[:])
+        nc.gpsimd.memset(neghalf[:], -0.5)
 
-        def load_scales(dst, src):
-            for q in range(4):
+        def load_scales(dst, src, lo, hi):
+            for r in range(4):
                 nc.sync.dma_start(
-                    out=dst[32 * q : 32 * q + 4, :, :].bitcast(I32),
-                    in_=src[:, 4 * q : 4 * q + 4, :].rearrange("g q n -> q g n").bitcast(I32),
+                    out=dst[r : P : 32, :, :].bitcast(I32),
+                    in_=src[:, r : 16 : 4, lo:hi].rearrange("g q n -> q g n").bitcast(I32),
                 )
 
         def load_words(dst, src, lo, hi):
             nc.sync.dma_start(out=dst[:], in_=src[:, :, 2 * lo : 2 * hi].rearrange("g p b -> p g b"))
 
-        load_scales(wo_sc, w_o_scales)
+        load_scales(wo_sc, w_o_scales, 0, D)
         load_words(wo, w_o_words, 0, D)
-        nc.scalar.dma_start(out=x_sb[:, 0, :], in_=x[0])
-        nc.sync.dma_start(out=a_bytes[:, 1, :], in_=attn_bytes[1])
-        load_scales(wg_sc, w_gate_scales)
-        load_scales(wu_sc, w_up_scales)
+        nc.sync.dma_start(out=a_bytes[:, 1:3, :], in_=attn_bytes[1:3].rearrange("i p d -> p i d"))
+        nc.sync.dma_start(out=x_sb[:, 0, :], in_=x[0])
+        nc.sync.dma_start(out=a_bytes[:, 3, :], in_=attn_bytes[3])
         wg = {}
         wu = {}
-        for lo, hi in ((0, 512), (512, 1024), (1024, 2048), (2048, 3072), (3072, 4096)):
+
+        def load_chunks(lo, hi):
             tg = keep.tile([P, 2, 2 * (hi - lo)], U8, align_bytes=64, name="wg" + str(lo))
             tu = keep.tile([P, 2, 2 * (hi - lo)], U8, align_bytes=64, name="wu" + str(lo))
             load_words(tg, w_gate_words, lo, hi)
@@ -104,12 +118,23 @@ def tile_transformerblocktpu_pb_w4_kernel(
             for c in range(lo // NC, hi // NC):
                 wg[c] = (tg, 2 * (NC * c - lo))
                 wu[c] = (tu, 2 * (NC * c - lo))
-            if lo == 512:
-                nc.sync.dma_start(out=x_sb[:, 1, :], in_=x[1])
-            if lo == 1024:
-                nc.sync.dma_start(out=a_bytes[:, 2:NT, :], in_=attn_bytes[2:NT].rearrange("i p d -> p i d"))
-        nc.sync.dma_start(out=x_sb[:, 2, :], in_=x[2])
-        nc.sync.dma_start(out=x_sb[:, 3, :], in_=x[3])
+
+        load_scales(wg_sc[0], w_gate_scales, 0, SPLIT)
+        load_scales(wu_sc[0], w_up_scales, 0, SPLIT)
+        load_chunks(0, 512)
+        load_chunks(512, 1024)
+        nc.sync.dma_start(out=x_sb[:, 1, :], in_=x[1])
+        load_chunks(1024, 2048)
+        load_chunks(2048, SPLIT)
+
+        def late_loads():
+            load_scales(wg_sc[1], w_gate_scales, SPLIT, M)
+            load_scales(wu_sc[1], w_up_scales, SPLIT, M)
+            load_chunks(SPLIT, 3072)
+            load_chunks(3072, 3584)
+            load_chunks(3584, 4096)
+            nc.sync.dma_start(out=x_sb[:, 2, :], in_=x[2])
+            nc.sync.dma_start(out=x_sb[:, 3, :], in_=x[3])
 
         abf = {}
         tbank = {}
@@ -120,7 +145,6 @@ def tile_transformerblocktpu_pb_w4_kernel(
         ss = {}
         rstd = {}
         hbf = {}
-        hbank = {}
         hgrp = {}
         hcod = {}
         hsca = {}
@@ -136,23 +160,22 @@ def tile_transformerblocktpu_pb_w4_kernel(
             else:
                 nc.scalar.copy(out=o, in_=s)
 
-        def turn_attn(i, g):
-            if i > 1 and g == 1:
-                tbank[(i, 1)] = tbank[(i, 0)][:, 1]
-            else:
-                b = bank([P, 2, 2, P])
-                tbank[(i, g)] = b[:, 0] if i <= 1 else b
-            dst = tbank[(i, g)] if i <= 1 or g == 1 else tbank[(i, g)][:, 0]
+        def turn_attn(i, g, dst):
             words = abf[i][:].bitcast(F32)
+            tbank[(i, g)] = dst
             for u in (0, 1):
                 nc.tensor.transpose(dst[:, u, :], words[:, 256 * g + u : 256 * (g + 1) : 2], ident[:])
+
+        def turn_attn_both(i, k):
+            b = bank([P, 2, 2, P], k)
+            turn_attn(i, 0, b[:, 0])
+            turn_attn(i, 1, b[:, 1])
 
         def scale_attn(i, g):
             if i not in agrp:
                 t = work.tile([P, 2, P, 2, 2], BF16, align_bytes=64, name="agrp")
                 agrp[i] = t
-            src = tbank[(i, g)] if i <= 1 or g == 1 else tbank[(i, g)][:, 0]
-            src = src.rearrange("p u r -> p (u r)").bitcast(BF16)
+            src = tbank[(i, g)].rearrange("p u r -> p (u r)").bitcast(BF16)
             src = src.rearrange("p (u r e) -> p r u e", u=2, e=2)
             sc = a_sc[:, g, :].rearrange("p (u e) -> p u e", u=2).unsqueeze(1).to_broadcast([P, P, 2, 2])
             nc.vector.tensor_tensor(out=agrp[i][:, g], in0=src, in1=sc, op=ALU.mult)
@@ -169,8 +192,8 @@ def tile_transformerblocktpu_pb_w4_kernel(
                 in_=agrp[i][:, lo:hi].rearrange("p g r u e -> p (g r u e)"),
             )
 
-        def mm1(i):
-            pbank[i] = [bank([P, NC]), bank([P, NC])]
+        def mm1(i, banks):
+            pbank[i] = banks
             for n in (0, 1):
                 for g in (0, 1):
                     nc.tensor.matmul_mx(
@@ -183,21 +206,25 @@ def tile_transformerblocktpu_pb_w4_kernel(
                         stop=(g == 1),
                     )
 
-        def add_x(i, n):
-            cols = slice(NC * n, NC * (n + 1))
-            nc.vector.tensor_tensor(out=xmid[i][:, cols], in0=pbank[i][n][:], in1=x_sb[:, i, cols], op=ALU.add)
+        def add_x(i, lo, hi):
+            n = lo // NC
+            nc.vector.tensor_tensor(
+                out=xmid[i][:, lo:hi], in0=pbank[i][n][:, lo - NC * n : hi - NC * n], in1=x_sb[:, i, lo:hi], op=ALU.add)
 
-        def square(i, n):
+        def square(i, k, lo, hi):
             if i not in ss:
-                t = work.tile([P, 2], F32, align_bytes=64, name="ss")
+                t = work.tile([P, 3], F32, align_bytes=64, name="ss")
                 ss[i] = t
-            cols = slice(NC * n, NC * (n + 1))
-            nc.scalar.activation(out=sqj[:], in_=xmid[i][:, cols], func=ACT.Square, scale=1.0 / 32.0, accum_out=ss[i][:, n : n + 1])
+            nc.scalar.activation(
+                out=sqj[:, : hi - lo], in_=xmid[i][:, lo:hi], func=ACT.Square, scale=1.0 / 32.0, accum_out=ss[i][:, k : k + 1])
 
-        def root(i):
+        def root_two(i):
             ms = work.tile([P, 1], F32, align_bytes=64, name="ms")
-            r = work.tile([P, 1], F32, align_bytes=64, name="rstd")
             nc.gpsimd.tensor_scalar(out=ms[:], in0=ss[i][:, 0:1], scalar1=ss[i][:, 1:2], scalar2=EPS, op0=ALU.add, op1=ALU.add)
+            return ms
+
+        def root_end(i, ms):
+            r = work.tile([P, 1], F32, align_bytes=64, name="rstd")
             nc.gpsimd.tensor_tensor(out=r[:], in0=ms[:], in1=neghalf[:], op=ALU.pow)
             rstd[i] = r
 
@@ -226,33 +253,38 @@ def tile_transformerblocktpu_pb_w4_kernel(
                 out=hbf[i][:, lo:hi].rearrange("q g u p e -> q (g u p e)"),
                 in0=ys[i][:, lo:hi].rearrange("q g k -> q (g k)"), scalar1=rstd[i][:], scalar2=None, op0=ALU.mult)
 
-        def turn_h(i, g):
-            b = bank([P, 2, P])
-            hbank[(i, g)] = b
+        def turn_h(i, g, b):
             words = hbf[i][:].rearrange("q g u p e -> q (g u p e)").bitcast(F32)
             for u in (0, 1):
                 nc.tensor.transpose(b[:, u, :], words[:, P * (2 * g + u) : P * (2 * g + u + 1)], ident[:])
 
-        def copy_h(i, g, on_vector):
+        def copy_h(i, lo, hi, b, on_vector):
             if i not in hgrp:
                 t = work.tile([P, 2, 4 * P], BF16, align_bytes=64, name="hgrp")
                 hgrp[i] = t
-            o = hgrp[i][:, g].bitcast(F32).rearrange("p (r u) -> p r u", u=2)
-            s = hbank[(i, g)][:].rearrange("p u r -> p r u")
+            o = hgrp[i][:, lo:hi].bitcast(F32).rearrange("p g (r u) -> p g r u", u=2)
+            s = b.rearrange("p g u r -> p g r u")
             if on_vector:
                 nc.vector.tensor_copy(out=o, in_=s)
             else:
                 nc.scalar.copy(out=o, in_=s)
 
-        def quant_h(i):
-            t = work.tile([P, 2 * P], U32, align_bytes=64, name="hcod")
-            t2 = work.tile([P, 2 * P], U8, align_bytes=64, name="hsca")
-            hcod[i], hsca[i] = t, t2
-            nc.vector.quantize_mx(out=t[:].bitcast(FP8X4), scales=t2[:], in_=hgrp[i][:].rearrange("p g w -> p (g w)"))
+        def quant_h(i, lo, hi):
+            if i not in hcod:
+                t = work.tile([P, 2 * P], U32, align_bytes=64, name="hcod")
+                t2 = work.tile([P, 2 * P], U8, align_bytes=64, name="hsca")
+                hcod[i], hsca[i] = t, t2
+            nc.vector.quantize_mx(
+                out=hcod[i][:, P * lo : P * hi].bitcast(FP8X4),
+                scales=hsca[i][:, P * lo : P * hi],
+                in_=hgrp[i][:, lo:hi].rearrange("p g w -> p (g w)"),
+            )
 
         def mm2(i, c, w, w_sc, lo, width):
-            b = bank([P, width])
+            b = next_bank([P, width])
             step = NC if width == NC else P
+            half = int(NC * c >= SPLIT)
+            first = NC * c - SPLIT * half
             for at_col in range(0, width, step):
               for g in (0, 1):
                 nc.tensor.matmul_mx(
@@ -260,7 +292,7 @@ def tile_transformerblocktpu_pb_w4_kernel(
                     lhsT=hcod[i][:, P * g : P * (g + 1)].bitcast(FP8X4),
                     lhsT_scale=hsca[i][:, P * g : P * (g + 1)],
                     rhs=w[c][0][:, g, w[c][1] + 2 * (lo + at_col) : w[c][1] + 2 * (lo + at_col + step)].bitcast(FP4X4),
-                    rhs_scale=w_sc[:, g, NC * c + lo + at_col : NC * c + lo + at_col + step],
+                    rhs_scale=w_sc[half][:, g, first + lo + at_col : first + lo + at_col + step],
                     start=(g == 0),
                     stop=(g == 1),
                 )
@@ -269,17 +301,18 @@ def tile_transformerblocktpu_pb_w4_kernel(
         def store_xmid(i):
             nc.sync.dma_start(out=out_0[i], in_=xmid[i][:])
 
-        def dummies(k):
-            b = bank([P, NC])
+        def dummies(k, b):
+            t = bank([P, NC], b)
             for j in range(k):
-                nc.tensor.matmul(b[:, :P], ones[:], ones[:], start=True, stop=True)
+                nc.tensor.matmul(t[:, :P], ones[:], ones[:], start=True, stop=True)
 
-        dummies(10)
+        dummies(22, 5)
         cast(0, 0, True)
         cast(0, 1, False)
-        turn_attn(0, 0)
-        turn_attn(0, 1)
-        gb = [bank([P, NC]), bank([P, NC])]
+        clear(wg_sc[1])
+        turn_attn(0, 0, bank([P, 2, P], 0))
+        turn_attn(0, 1, bank([P, 2, P], 1))
+        gb = [bank([P, NC], 2), bank([P, NC], 3)]
         for n in (0, 1):
             nc.tensor.matmul(gb[n][:], ones[:], gain_row[:, NC * n : NC * (n + 1)], start=True, stop=True)
         for n in (0, 1):
@@ -288,52 +321,72 @@ def tile_transformerblocktpu_pb_w4_kernel(
         scale_attn(0, 1)
         quant_attn(0, 0, 1)
         quant_attn(0, 1, 2)
-        mm1(0)
-        cast(1, 0, False)
-        cast(1, 1, False)
-        add_x(0, 0)
-        square(0, 0)
-        add_x(0, 1)
-        square(0, 1)
-        root(0)
-        turn_attn(1, 0)
-        turn_attn(1, 1)
+        dummies(5, 5)
+        mm1(0, [bank([P, NC], 0), bank([P, NC], 1)])
+        cast(1, 0, True)
+        cast(1, 1, True)
+        cast(2, 0, False)
+        cast(2, 1, False)
+        add_x(0, 0, 512)
+        square(0, 0, 0, 512)
+        add_x(0, 512, 768)
+        square(0, 1, 512, 768)
+        ms0 = root_two(0)
+        add_x(0, 768, 1024)
+        square(0, 2, 768, 1024)
+        ms1 = work.tile([P, 1], F32, align_bytes=64, name="ms")
+        nc.gpsimd.tensor_tensor(out=ms1[:], in0=ms0[:], in1=ss[0][:, 2:3], op=ALU.add)
+        root_end(0, ms1)
+        turn_attn_both(1, 4)
+        turn_attn_both(2, 7)
+        dummies(8, 2)
+        cast(3, 0, False)
+        cast(3, 1, False)
         gain_y(0, 0, nc.vector)
         gain_y(0, 1, nc.vector)
         h_norm(0, 0, 1)
         h_norm(0, 1, 2)
-        turn_h(0, 0)
-        turn_h(0, 1)
+        hb = [bank([P, 1, 2, P], 6), bank([P, 1, 2, P], 3)]
+        turn_h(0, 0, hb[0][:, 0])
+        turn_h(0, 1, hb[1][:, 0])
+        clear(wu_sc[1])
+        copy_h(0, 0, 1, hb[0], False)
+        copy_h(0, 1, 2, hb[1], True)
+        quant_h(0, 0, 1)
+        quant_h(0, 1, 2)
+        dummies(4, 2)
         scale_attn(1, 0)
-        copy_h(0, 0, False)
-        copy_h(0, 1, True)
-        dummies(8)
-        quant_h(0)
         scale_attn(1, 1)
         quant_attn(1, 0, 2)
+        late_loads()
+
+        def turn_and_copy_h(i, k):
+            b = bank([P, 2, 2, P], k)
+            turn_h(i, 0, b[:, 0])
+            turn_h(i, 1, b[:, 1])
+            copy_h(i, 0, 2, b, False)
 
         at = {}
 
         def put(pos, *fs):
             at.setdefault(pos, []).extend(fs)
 
-        def plan_attn(i, pos):
-            put(pos, lambda: cast(i, 0, False), lambda: cast(i, 1, False))
-            put(pos + 1, lambda: (turn_attn(i, 0), turn_attn(i, 1)), lambda: scale_attn(i, 0))
-            put(pos + 2, lambda: scale_attn(i, 1), lambda: quant_attn(i, 0, 2))
-
-        def plan_rest(i, pos):
-            put(pos, lambda: mm1(i), lambda: add_x(i, 0))
-            put(pos + 1, lambda: add_x(i, 1), lambda: square(i, 0), lambda: gain_y(i, 0, nc.gpsimd))
-            put(pos + 2, lambda: square(i, 1), lambda: gain_y(i, 1, nc.gpsimd), lambda: root(i), lambda: store_xmid(i))
+        def plan_rest(i, pos, k):
+            put(pos, lambda: mm1(i, [next_bank([P, NC]), next_bank([P, NC])]), lambda: add_x(i, 0, 512))
+            put(pos + 1, lambda: add_x(i, 512, 1024), lambda: square(i, 0, 0, 512), lambda: gain_y(i, 0, nc.gpsimd))
+            put(pos + 2, lambda: square(i, 1, 512, 1024), lambda: gain_y(i, 1, nc.gpsimd), lambda: root_end(i, root_two(i)), lambda: store_xmid(i))
             put(pos + 4, lambda: h_norm(i, 0, 2))
-            put(pos + 6, lambda: (turn_h(i, 0), turn_h(i, 1), copy_h(i, 0, False), copy_h(i, 1, False)), lambda: quant_h(i))
+            put(pos + 6, lambda: turn_and_copy_h(i, k), lambda: quant_h(i, 0, 2))
 
-        plan_rest(1, 0)
-        plan_attn(2, 3)
-        plan_rest(2, 7)
-        plan_attn(3, 10)
-        plan_rest(3, 15)
+        put(6, lambda: turn_attn_both(3, 7))
+        plan_rest(1, 0, 6)
+        put(2, lambda: scale_attn(2, 0))
+        put(3, lambda: scale_attn(2, 1))
+        put(5, lambda: quant_attn(2, 0, 2))
+        plan_rest(2, 7, 6)
+        put(9, lambda: scale_attn(3, 0))
+        put(10, lambda: scale_attn(3, 1), lambda: quant_attn(3, 0, 2))
+        plan_rest(3, 15, 7)
 
         for i in range(NT):
             for c in range(CHUNKS):

@@ -21,7 +21,8 @@ NT = 4
 EPS = 1e-6
 NC = 512
 CHUNKS = M // NC
-SPLIT = 5 * NC
+PL = {'m1': 0, 'a1': 0, 'yv': 1, 'y0': 0, 'y1': 0, 'h': 2, 't': 4, 'qh': 4, 's2': 5, 's2b': 6, 'c3': 6, 't3': 9, 'b3': 6, 'r2': 8, 's3': 9, 'r3': 15, 'st0': 9, 'd1': 4, 'd2': 12, 'd3': 6}
+SPLIT = 6 * NC
 
 FLOPS = 2 * NT * P * D * (D + 2 * M)
 
@@ -106,7 +107,6 @@ def tile_transformerblocktpu_pb_w4_kernel(
         load_words(wo, w_o_words, 0, D)
         nc.sync.dma_start(out=a_bytes[:, 1:3, :], in_=attn_bytes[1:3].rearrange("i p d -> p i d"))
         nc.sync.dma_start(out=x_sb[:, 0, :], in_=x[0])
-        nc.sync.dma_start(out=a_bytes[:, 3, :], in_=attn_bytes[3])
         wg = {}
         wu = {}
 
@@ -125,14 +125,13 @@ def tile_transformerblocktpu_pb_w4_kernel(
         load_chunks(512, 1024)
         nc.sync.dma_start(out=x_sb[:, 1, :], in_=x[1])
         load_chunks(1024, 2048)
-        load_chunks(2048, SPLIT)
+        load_chunks(2048, 3072)
 
         def late_loads():
             load_scales(wg_sc[1], w_gate_scales, SPLIT, M)
             load_scales(wu_sc[1], w_up_scales, SPLIT, M)
-            load_chunks(SPLIT, 3072)
-            load_chunks(3072, 3584)
-            load_chunks(3584, 4096)
+            load_chunks(3072, 4096)
+            nc.sync.dma_start(out=a_bytes[:, 3, :], in_=attn_bytes[3])
             nc.sync.dma_start(out=x_sb[:, 2, :], in_=x[2])
             nc.sync.dma_start(out=x_sb[:, 3, :], in_=x[3])
 
@@ -321,7 +320,7 @@ def tile_transformerblocktpu_pb_w4_kernel(
         scale_attn(0, 1)
         quant_attn(0, 0, 1)
         quant_attn(0, 1, 2)
-        dummies(5, 5)
+        dummies(PL["d1"], 5)
         mm1(0, [bank([P, NC], 0), bank([P, NC], 1)])
         cast(1, 0, True)
         cast(1, 1, True)
@@ -339,9 +338,7 @@ def tile_transformerblocktpu_pb_w4_kernel(
         root_end(0, ms1)
         turn_attn_both(1, 4)
         turn_attn_both(2, 7)
-        dummies(8, 2)
-        cast(3, 0, False)
-        cast(3, 1, False)
+        dummies(PL["d2"], 2)
         gain_y(0, 0, nc.vector)
         gain_y(0, 1, nc.vector)
         h_norm(0, 0, 1)
@@ -354,7 +351,7 @@ def tile_transformerblocktpu_pb_w4_kernel(
         copy_h(0, 1, 2, hb[1], True)
         quant_h(0, 0, 1)
         quant_h(0, 1, 2)
-        dummies(4, 2)
+        dummies(PL["d3"], 2)
         scale_attn(1, 0)
         scale_attn(1, 1)
         quant_attn(1, 0, 2)
@@ -378,21 +375,31 @@ def tile_transformerblocktpu_pb_w4_kernel(
             put(pos + 4, lambda: h_norm(i, 0, 2))
             put(pos + 6, lambda: turn_and_copy_h(i, k), lambda: quant_h(i, 0, 2))
 
-        put(6, lambda: turn_attn_both(3, 7))
-        plan_rest(1, 0, 6)
-        put(2, lambda: scale_attn(2, 0))
-        put(3, lambda: scale_attn(2, 1))
-        put(5, lambda: quant_attn(2, 0, 2))
-        plan_rest(2, 7, 6)
-        put(9, lambda: scale_attn(3, 0))
-        put(10, lambda: scale_attn(3, 1), lambda: quant_attn(3, 0, 2))
-        plan_rest(3, 15, 7)
+        put(PL["m1"], lambda: mm1(1, [next_bank([P, NC]), next_bank([P, NC])]), lambda: add_x(1, 0, 512), lambda: square(1, 0, 0, 512))
+        put(PL["a1"], lambda: add_x(1, 512, 1024), lambda: square(1, 1, 512, 1024), lambda: root_end(1, root_two(1)))
+        eng = nc.vector if PL["yv"] else nc.gpsimd
+        put(PL["y0"], lambda: gain_y(1, 0, eng))
+        put(PL["y1"], lambda: gain_y(1, 1, eng))
+        put(PL["h"], lambda: h_norm(1, 0, 2))
+        put(PL["t"], lambda: turn_and_copy_h(1, 6))
+        put(PL["qh"], lambda: quant_h(1, 0, 2))
+        put(PL["s2"], lambda: store_xmid(1), lambda: scale_attn(2, 0))
+        put(PL["s2b"], lambda: scale_attn(2, 1), lambda: quant_attn(2, 0, 2))
+        put(PL["c3"], lambda: cast(3, 0, False))
+        put(PL["c3"] + 1, lambda: cast(3, 1, False))
+        put(PL["t3"], lambda: turn_attn_both(3, PL["b3"]))
+        plan_rest(2, PL["r2"], 7)
+        put(PL["s3"], lambda: scale_attn(3, 0))
+        put(PL["s3"] + 1, lambda: scale_attn(3, 1), lambda: quant_attn(3, 0, 2))
+        plan_rest(3, PL["r3"], 6)
 
-        for i in range(NT):
-            for c in range(CHUNKS):
+        sequence = [(i, c) for i in (0, 1) for c in range(6)]
+        sequence += [(i, c) for i in (0, 1) for c in range(6, CHUNKS)]
+        sequence += [(i, c) for i in (2, 3) for c in range(CHUNKS)]
+        for pos, (i, c) in enumerate(sequence):
                 last = i == NT - 1 and c == CHUNKS - 1
-                width = NC // 2 if last else NC
-                for lo in range(0, NC, width):
+                pieces = ((0, 256), (256, 128), (384, 128)) if last else ((0, NC),)
+                for lo, width in pieces:
                     bg = mm2(i, c, wg, wg_sc, lo, width)
                     bu = mm2(i, c, wu, wu_sc, lo, width)
                     s = work.tile([P, NC], F32, align_bytes=64, name="s")
@@ -401,7 +408,7 @@ def tile_transformerblocktpu_pb_w4_kernel(
                     nc.vector.tensor_tensor(out=o[:, :width], in0=bu[:], in1=s[:, :width], op=ALU.mult)
                     first = NC * c + lo
                     nc.sync.dma_start(out=out_1[i, :, first : first + width], in_=o[:, :width])
-                if i == 0 and c == 0:
+                if pos == PL["st0"]:
                     store_xmid(0)
-                for step in at.get(CHUNKS * i + c, []):
+                for step in at.get(pos, []):
                     step()

@@ -21,7 +21,7 @@ NT = 4
 EPS = 1e-6
 NC = 512
 CHUNKS = M // NC
-PL = {'m1': 0, 'a1': 0, 'yv': 1, 'y0': 0, 'y1': 0, 'h': 2, 't': 4, 'qh': 4, 's2': 5, 's2b': 6, 'c3': 6, 't3': 9, 'b3': 6, 'r2': 8, 's3': 9, 'r3': 15, 'st0': 9, 'd1': 4, 'd2': 12, 'd3': 6}
+PL = {'m1': 0, 'a1': 0, 'yv': 1, 'y0': 0, 'y1': 0, 'h': 2, 't': 4, 'qh': 4, 's2': 5, 's2b': 6, 'c3': 6, 't3': 9, 'b3': 6, 'r2': 8, 's3': 9, 'r3': 15, 'st0': 9, 'd1': 4, 'd2': 16, 'd3': 7}
 SPLIT = 6 * NC
 
 FLOPS = 2 * NT * P * D * (D + 2 * M)
@@ -61,14 +61,14 @@ def tile_transformerblocktpu_pb_w4_kernel(
         gain_row = keep.tile([P, D], BF16, align_bytes=64, name="gain_row")
         gain = keep.tile([P, D], BF16, align_bytes=64, name="gain")
         neghalf = keep.tile([P, 1], F32, align_bytes=64, name="neghalf")
-        warm = keep.tile([P, 2], F32, align_bytes=64, name="warm")
+        warm = keep.tile([P, 3], F32, align_bytes=64, name="warm")
         xmid = []
         for i in range(NT):
             t = keep.tile([P, D], F32, align_bytes=64, name="xmid" + str(i))
             xmid.append(t)
         sqj = keep.tile([P, NC], F32, align_bytes=64, name="sqj")
 
-        nc.gpsimd.memset(warm[:, 0:1], 0.0)
+        nc.gpsimd.memset(warm[:, 0:1], 1.0)
         nc.gpsimd.memset(ones[:], 1.0)
         nc.vector.memset(gain_row[:].bitcast(I32), 0)
         nc.vector.memset(wo_sc[:].rearrange("p g n -> p (g n)").bitcast(I32), 0)
@@ -89,7 +89,7 @@ def tile_transformerblocktpu_pb_w4_kernel(
         nc.sync.dma_start(out=a_bytes[:, 0, :], in_=attn_bytes[0])
         nc.scalar.dma_start(out=a_sc[:], in_=attn_scale.rearrange("a b (g p t) -> p (a b g) t", p=P, t=4))
         nc.scalar.dma_start(out=gain_row[0:1, :], in_=rms2_scale.unsqueeze(0))
-        nc.scalar.activation(out=warm[:, 1:2], in_=warm[:, 0:1], func=ACT.Silu)
+        nc.scalar.activation(out=warm[:, 1:2], in_=warm[:, 0:1], func=ACT.Abs_reciprocal_sqrt)
         make_identity(nc, ident[:])
         nc.gpsimd.memset(neghalf[:], -0.5)
 
@@ -308,7 +308,9 @@ def tile_transformerblocktpu_pb_w4_kernel(
         dummies(22, 5)
         cast(0, 0, True)
         cast(0, 1, False)
-        clear(wg_sc[1])
+        nc.gpsimd.tensor_copy(out=warm[:, 2:3], in_=abf[0][:, 0:1])
+        for t in (wg_sc[1], wu_sc[1]):
+            nc.gpsimd.memset(t[:].rearrange("p g n -> p (g n)").bitcast(I32), 0)
         turn_attn(0, 0, bank([P, 2, P], 0))
         turn_attn(0, 1, bank([P, 2, P], 1))
         gb = [bank([P, NC], 2), bank([P, NC], 3)]
@@ -333,9 +335,9 @@ def tile_transformerblocktpu_pb_w4_kernel(
         ms0 = root_two(0)
         add_x(0, 768, 1024)
         square(0, 2, 768, 1024)
-        ms1 = work.tile([P, 1], F32, align_bytes=64, name="ms")
-        nc.gpsimd.tensor_tensor(out=ms1[:], in0=ms0[:], in1=ss[0][:, 2:3], op=ALU.add)
-        root_end(0, ms1)
+        r0 = work.tile([P, 1], F32, align_bytes=64, name="rstd")
+        nc.scalar.activation(out=r0[:], in_=ss[0][:, 2:3], func=ACT.Abs_reciprocal_sqrt, bias=ms0[:])
+        rstd[0] = r0
         turn_attn_both(1, 4)
         turn_attn_both(2, 7)
         dummies(PL["d2"], 2)
@@ -346,13 +348,13 @@ def tile_transformerblocktpu_pb_w4_kernel(
         hb = [bank([P, 1, 2, P], 6), bank([P, 1, 2, P], 3)]
         turn_h(0, 0, hb[0][:, 0])
         turn_h(0, 1, hb[1][:, 0])
-        clear(wu_sc[1])
+        scale_attn(1, 0)
         copy_h(0, 0, 1, hb[0], False)
+        nc.scalar.activation(out=warm[:, 1:2], in_=warm[:, 0:1], func=ACT.Silu)
         copy_h(0, 1, 2, hb[1], True)
         quant_h(0, 0, 1)
         quant_h(0, 1, 2)
         dummies(PL["d3"], 2)
-        scale_attn(1, 0)
         scale_attn(1, 1)
         quant_attn(1, 0, 2)
         late_loads()

@@ -21,7 +21,7 @@ NT = 4
 EPS = 1e-6
 NC = 512
 CHUNKS = M // NC
-PL = {'m1': 0, 'a1': 0, 'yv': 1, 'y0': 0, 'y1': 0, 'h': 2, 't': 4, 'qh': 4, 's2': 5, 's2b': 6, 'c3': 6, 't3': 9, 'b3': 6, 'r2': 8, 's3': 9, 'r3': 15, 'st0': 9, 'd1': 4, 'd2': 16, 'd3': 7}
+PL = {'m1': 0, 'a1': 0, 'yv': 1, 'y0': 0, 'y1': 0, 'h': 2, 't': 4, 'qh': 4, 's2': 5, 's2b': 6, 'c3': 2, 't3': 9, 'b3': 6, 'r2': 8, 's3': 9, 'r3': 15, 'st0': 9, 'd1': 4, 'd2': 20, 'd3': 10}
 SPLIT = 6 * NC
 
 FLOPS = 2 * NT * P * D * (D + 2 * M)
@@ -51,22 +51,22 @@ def tile_transformerblocktpu_pb_w4_kernel(
             count[0] += 1
             return bank(shape, order[n] if n < len(order) else (n - len(order)) % 6)
 
-        a_bytes = keep.tile([P, NT, D], U8, align_bytes=64, name="a_bytes")
-        a_sc = keep.tile([P, 2, 4], F32, align_bytes=64, name="a_sc")
-        x_sb = keep.tile([P, NT, D], BF16, align_bytes=64, name="x_sb")
-        wo = keep.tile([P, 2, 2 * D], U8, align_bytes=64, name="wo")
-        wo_sc = keep.tile([P, 2, D], U8, align_bytes=64, name="wo_sc")
-        ident = keep.tile([P, P], F32, align_bytes=64, name="ident")
-        ones = keep.tile([P, P], BF16, align_bytes=64, name="ones")
-        gain_row = keep.tile([P, D], BF16, align_bytes=64, name="gain_row")
-        gain = keep.tile([P, D], BF16, align_bytes=64, name="gain")
-        neghalf = keep.tile([P, 1], F32, align_bytes=64, name="neghalf")
-        warm = keep.tile([P, 3], F32, align_bytes=64, name="warm")
+        a_bytes = keep.tile([P, NT, D], U8, align_bytes=256, name="a_bytes")
+        a_sc = keep.tile([P, 2, 4], F32, align_bytes=256, name="a_sc")
+        x_sb = keep.tile([P, NT, D], BF16, align_bytes=256, name="x_sb")
+        wo = keep.tile([P, 2, 2 * D], U8, align_bytes=256, name="wo")
+        wo_sc = keep.tile([P, 2, D], U8, align_bytes=256, name="wo_sc")
+        ident = keep.tile([P, P], F32, align_bytes=256, name="ident")
+        ones = keep.tile([P, P], BF16, align_bytes=256, name="ones")
+        gain_row = keep.tile([P, D], BF16, align_bytes=256, name="gain_row")
+        gain = keep.tile([P, D], BF16, align_bytes=256, name="gain")
+        neghalf = keep.tile([P, 1], F32, align_bytes=256, name="neghalf")
+        warm = keep.tile([P, 3], F32, align_bytes=256, name="warm")
         xmid = []
         for i in range(NT):
-            t = keep.tile([P, D], F32, align_bytes=64, name="xmid" + str(i))
+            t = keep.tile([P, D], F32, align_bytes=256, name="xmid" + str(i))
             xmid.append(t)
-        sqj = keep.tile([P, NC], F32, align_bytes=64, name="sqj")
+        sqj = keep.tile([P, NC], F32, align_bytes=256, name="sqj")
 
         nc.gpsimd.memset(warm[:, 0:1], 1.0)
         nc.gpsimd.memset(ones[:], 1.0)
@@ -75,9 +75,9 @@ def tile_transformerblocktpu_pb_w4_kernel(
         wg_sc = []
         wu_sc = []
         for half, width in ((0, SPLIT), (1, M - SPLIT)):
-            t = keep.tile([P, 2, width], U8, align_bytes=64, name="wg_sc" + str(half))
+            t = keep.tile([P, 2, width], U8, align_bytes=256, name="wg_sc" + str(half))
             wg_sc.append(t)
-            t2 = keep.tile([P, 2, width], U8, align_bytes=64, name="wu_sc" + str(half))
+            t2 = keep.tile([P, 2, width], U8, align_bytes=256, name="wu_sc" + str(half))
             wu_sc.append(t2)
 
         def clear(t):
@@ -111,8 +111,8 @@ def tile_transformerblocktpu_pb_w4_kernel(
         wu = {}
 
         def load_chunks(lo, hi):
-            tg = keep.tile([P, 2, 2 * (hi - lo)], U8, align_bytes=64, name="wg" + str(lo))
-            tu = keep.tile([P, 2, 2 * (hi - lo)], U8, align_bytes=64, name="wu" + str(lo))
+            tg = keep.tile([P, 2, 2 * (hi - lo)], U8, align_bytes=256, name="wg" + str(lo))
+            tu = keep.tile([P, 2, 2 * (hi - lo)], U8, align_bytes=256, name="wu" + str(lo))
             load_words(tg, w_gate_words, lo, hi)
             load_words(tu, w_up_words, lo, hi)
             for c in range(lo // NC, hi // NC):
@@ -125,13 +125,13 @@ def tile_transformerblocktpu_pb_w4_kernel(
         load_chunks(512, 1024)
         nc.sync.dma_start(out=x_sb[:, 1, :], in_=x[1])
         load_chunks(1024, 2048)
+        nc.sync.dma_start(out=a_bytes[:, 3, :], in_=attn_bytes[3])
         load_chunks(2048, 3072)
 
         def late_loads():
             load_scales(wg_sc[1], w_gate_scales, SPLIT, M)
             load_scales(wu_sc[1], w_up_scales, SPLIT, M)
             load_chunks(3072, 4096)
-            nc.sync.dma_start(out=a_bytes[:, 3, :], in_=attn_bytes[3])
             nc.sync.dma_start(out=x_sb[:, 2, :], in_=x[2])
             nc.sync.dma_start(out=x_sb[:, 3, :], in_=x[3])
 
@@ -150,7 +150,7 @@ def tile_transformerblocktpu_pb_w4_kernel(
 
         def cast(i, g, on_vector):
             if i not in abf:
-                t = work.tile([P, D], BF16, align_bytes=64, name="abf")
+                t = work.tile([P, D], BF16, align_bytes=256, name="abf")
                 abf[i] = t
             o = abf[i][:, NC * g : NC * (g + 1)]
             s = a_bytes[:, i, NC * g : NC * (g + 1)].bitcast(F8)
@@ -172,7 +172,7 @@ def tile_transformerblocktpu_pb_w4_kernel(
 
         def scale_attn(i, g):
             if i not in agrp:
-                t = work.tile([P, 2, P, 2, 2], BF16, align_bytes=64, name="agrp")
+                t = work.tile([P, 2, P, 2, 2], BF16, align_bytes=256, name="agrp")
                 agrp[i] = t
             src = tbank[(i, g)].rearrange("p u r -> p (u r)").bitcast(BF16)
             src = src.rearrange("p (u r e) -> p r u e", u=2, e=2)
@@ -181,9 +181,9 @@ def tile_transformerblocktpu_pb_w4_kernel(
 
         def quant_attn(i, lo, hi):
             if i not in acod:
-                t = work.tile([P, 2 * P], U32, align_bytes=64, name="acod")
+                t = work.tile([P, 2 * P], U32, align_bytes=256, name="acod")
                 acod[i] = t
-                t2 = work.tile([P, 2 * P], U8, align_bytes=64, name="asca")
+                t2 = work.tile([P, 2 * P], U8, align_bytes=256, name="asca")
                 asca[i] = t2
             nc.vector.quantize_mx(
                 out=acod[i][:, P * lo : P * hi].bitcast(FP8X4),
@@ -212,18 +212,18 @@ def tile_transformerblocktpu_pb_w4_kernel(
 
         def square(i, k, lo, hi):
             if i not in ss:
-                t = work.tile([P, 3], F32, align_bytes=64, name="ss")
+                t = work.tile([P, 3], F32, align_bytes=256, name="ss")
                 ss[i] = t
             nc.scalar.activation(
                 out=sqj[:, : hi - lo], in_=xmid[i][:, lo:hi], func=ACT.Square, scale=1.0 / 32.0, accum_out=ss[i][:, k : k + 1])
 
         def root_two(i):
-            ms = work.tile([P, 1], F32, align_bytes=64, name="ms")
+            ms = work.tile([P, 1], F32, align_bytes=256, name="ms")
             nc.gpsimd.tensor_scalar(out=ms[:], in0=ss[i][:, 0:1], scalar1=ss[i][:, 1:2], scalar2=EPS, op0=ALU.add, op1=ALU.add)
             return ms
 
         def root_end(i, ms):
-            r = work.tile([P, 1], F32, align_bytes=64, name="rstd")
+            r = work.tile([P, 1], F32, align_bytes=256, name="rstd")
             nc.gpsimd.tensor_tensor(out=r[:], in0=ms[:], in1=neghalf[:], op=ALU.pow)
             rstd[i] = r
 
@@ -232,14 +232,14 @@ def tile_transformerblocktpu_pb_w4_kernel(
 
         def h_tile(i):
             if i not in hbf:
-                t = work.tile([P, 2, 2, P, 2], BF16, align_bytes=64, name="hbf")
+                t = work.tile([P, 2, 2, P, 2], BF16, align_bytes=256, name="hbf")
                 hbf[i] = t
 
         ys = {}
 
         def gain_y(i, g, engine):
             if i not in ys:
-                t = work.tile([P, 2, NC], F32, align_bytes=64, name="y", bufs=2)
+                t = work.tile([P, 2, NC], F32, align_bytes=256, name="y", bufs=2)
                 ys[i] = t
             cols = slice(NC * g, NC * (g + 1))
             engine.tensor_tensor(
@@ -259,7 +259,7 @@ def tile_transformerblocktpu_pb_w4_kernel(
 
         def copy_h(i, lo, hi, b, on_vector):
             if i not in hgrp:
-                t = work.tile([P, 2, 4 * P], BF16, align_bytes=64, name="hgrp")
+                t = work.tile([P, 2, 4 * P], BF16, align_bytes=256, name="hgrp")
                 hgrp[i] = t
             o = hgrp[i][:, lo:hi].bitcast(F32).rearrange("p g (r u) -> p g r u", u=2)
             s = b.rearrange("p g u r -> p g r u")
@@ -270,8 +270,8 @@ def tile_transformerblocktpu_pb_w4_kernel(
 
         def quant_h(i, lo, hi):
             if i not in hcod:
-                t = work.tile([P, 2 * P], U32, align_bytes=64, name="hcod")
-                t2 = work.tile([P, 2 * P], U8, align_bytes=64, name="hsca")
+                t = work.tile([P, 2 * P], U32, align_bytes=256, name="hcod")
+                t2 = work.tile([P, 2 * P], U8, align_bytes=256, name="hsca")
                 hcod[i], hsca[i] = t, t2
             nc.vector.quantize_mx(
                 out=hcod[i][:, P * lo : P * hi].bitcast(FP8X4),
@@ -335,7 +335,7 @@ def tile_transformerblocktpu_pb_w4_kernel(
         ms0 = root_two(0)
         add_x(0, 768, 1024)
         square(0, 2, 768, 1024)
-        r0 = work.tile([P, 1], F32, align_bytes=64, name="rstd")
+        r0 = work.tile([P, 1], F32, align_bytes=256, name="rstd")
         nc.scalar.activation(out=r0[:], in_=ss[0][:, 2:3], func=ACT.Abs_reciprocal_sqrt, bias=ms0[:])
         rstd[0] = r0
         turn_attn_both(1, 4)
@@ -360,7 +360,7 @@ def tile_transformerblocktpu_pb_w4_kernel(
         late_loads()
 
         def turn_and_copy_h(i, k):
-            b = bank([P, 2, 2, P], k)
+            b = next_bank([P, 2, 2, P]) if k is None else bank([P, 2, 2, P], k)
             turn_h(i, 0, b[:, 0])
             turn_h(i, 1, b[:, 1])
             copy_h(i, 0, 2, b, False)
@@ -383,13 +383,12 @@ def tile_transformerblocktpu_pb_w4_kernel(
         put(PL["y0"], lambda: gain_y(1, 0, eng))
         put(PL["y1"], lambda: gain_y(1, 1, eng))
         put(PL["h"], lambda: h_norm(1, 0, 2))
-        put(PL["t"], lambda: turn_and_copy_h(1, 6))
+        put(PL["t"], lambda: turn_and_copy_h(1, None), lambda: turn_attn_both(3, 6))
         put(PL["qh"], lambda: quant_h(1, 0, 2))
         put(PL["s2"], lambda: store_xmid(1), lambda: scale_attn(2, 0))
         put(PL["s2b"], lambda: scale_attn(2, 1), lambda: quant_attn(2, 0, 2))
         put(PL["c3"], lambda: cast(3, 0, False))
         put(PL["c3"] + 1, lambda: cast(3, 1, False))
-        put(PL["t3"], lambda: turn_attn_both(3, PL["b3"]))
         plan_rest(2, PL["r2"], 7)
         put(PL["s3"], lambda: scale_attn(3, 0))
         put(PL["s3"] + 1, lambda: scale_attn(3, 1), lambda: quant_attn(3, 0, 2))
@@ -404,9 +403,9 @@ def tile_transformerblocktpu_pb_w4_kernel(
                 for lo, width in pieces:
                     bg = mm2(i, c, wg, wg_sc, lo, width)
                     bu = mm2(i, c, wu, wu_sc, lo, width)
-                    s = work.tile([P, NC], F32, align_bytes=64, name="s")
+                    s = work.tile([P, NC], F32, align_bytes=256, name="s")
                     nc.scalar.activation(out=s[:, :width], in_=bg[:], func=ACT.Silu)
-                    o = outp.tile([P, NC], F32, align_bytes=64, name="o")
+                    o = outp.tile([P, NC], F32, align_bytes=256, name="o")
                     nc.vector.tensor_tensor(out=o[:, :width], in0=bu[:], in1=s[:, :width], op=ALU.mult)
                     first = NC * c + lo
                     nc.sync.dma_start(out=out_1[i, :, first : first + width], in_=o[:, :width])

from contextlib import ExitStack

import concourse.mybir as mybir
from concourse.masks import make_identity

F32 = mybir.dt.float32
BF16 = mybir.dt.bfloat16
I32 = mybir.dt.int32
U32 = mybir.dt.uint32
U8 = mybir.dt.uint8
F8 = mybir.dt.float8_e4m3fn
FP8X4 = mybir.dt.float8_e4m3fn_x4
FP4X4 = mybir.dt.float4_e2m1fn_x4
ACT = mybir.ActivationFunctionType
ALU = mybir.AluOpType

P = 128
D = 1024
M = 4096
NT = 4
EPS = 1e-6
NC = 512
CHUNKS = M // NC
PL = {'m1': 0, 'a1': 0, 'yv': 1, 'y0': 0, 'y1': 0, 'h': 2, 't': 4, 'qh': 4, 's2': 5, 's2b': 6, 'c3': 2, 't3': 9, 'b3': 6, 'r2': 8, 's3': 9, 'r3': 15, 'st0': 9, 'd1': 4, 'd2': 20, 'd3': 10}
SPLIT = 6 * NC

FLOPS = 2 * NT * P * D * (D + 2 * M)


def tile_transformerblocktpu_pb_w4_kernel(
    tc, attn_bytes, attn_scale, x, w_o_words, w_o_scales, rms2_scale,
    w_gate_words, w_gate_scales, w_up_words, w_up_scales, out_0, out_1,
):
    nc = tc.nc
    with ExitStack() as ctx:
        keep = ctx.enter_context(tc.tile_pool(name="keep", bufs=1))
        work = ctx.enter_context(tc.tile_pool(name="work", bufs=4))
        outp = ctx.enter_context(tc.tile_pool(name="outp", bufs=10))
        psum = ctx.enter_context(tc.psum_pool(name="psum", bufs=1))
        ctx.enter_context(tc.manual_schedule())

        order = [0, 1, 2, 3, 5, 0, 1, 2, 3, 4, 5]
        count = [0]

        def bank(shape, k):
            b = psum.tile(shape, F32, name="bank" + str(k), tag="bank" + str(k))
            return b

        def next_bank(shape):
            n = count[0]
            count[0] += 1
            return bank(shape, order[n] if n < len(order) else (n - len(order)) % 6)

        a_bytes = keep.tile([P, NT, D], U8, align_bytes=256, name="a_bytes")
        a_sc = keep.tile([P, 2, 4], F32, align_bytes=256, name="a_sc")
        x_sb = keep.tile([P, NT, D], BF16, align_bytes=256, name="x_sb")
        wo = keep.tile([P, 2, 2 * D], U8, align_bytes=256, name="wo")
        wo_sc = keep.tile([P, 2, D], U8, align_bytes=256, name="wo_sc")
        ident = keep.tile([P, P], F32, align_bytes=256, name="ident")
        ones = keep.tile([P, P], BF16, align_bytes=256, name="ones")
        gain_row = keep.tile([P, D], BF16, align_bytes=256, name="gain_row")
        gain = keep.tile([P, D], BF16, align_bytes=256, name="gain")
        neghalf = keep.tile([P, 1], F32, align_bytes=256, name="neghalf")
        warm = keep.tile([P, 3], F32, align_bytes=256, name="warm")
        xmid = []
        for i in range(NT):
            t = keep.tile([P, D], F32, align_bytes=256, name="xmid" + str(i))
            xmid.append(t)
        sqj = keep.tile([P, NC], F32, align_bytes=256, name="sqj")

        nc.gpsimd.memset(warm[:, 0:1], 1.0)
        nc.gpsimd.memset(ones[:], 1.0)
        nc.vector.memset(gain_row[:].bitcast(I32), 0)
        nc.vector.memset(wo_sc[:].rearrange("p g n -> p (g n)").bitcast(I32), 0)
        wg_sc = []
        wu_sc = []
        for half, width in ((0, SPLIT), (1, M - SPLIT)):
            t = keep.tile([P, 2, width], U8, align_bytes=256, name="wg_sc" + str(half))
            wg_sc.append(t)
            t2 = keep.tile([P, 2, width], U8, align_bytes=256, name="wu_sc" + str(half))
            wu_sc.append(t2)

        def clear(t):
            nc.vector.memset(t[:].rearrange("p g n -> p (g n)").bitcast(I32), 0)

        clear(wg_sc[0])
        clear(wu_sc[0])

        nc.sync.dma_start(out=a_bytes[:, 0, :], in_=attn_bytes[0])
        nc.scalar.dma_start(out=a_sc[:], in_=attn_scale.rearrange("a b (g p t) -> p (a b g) t", p=P, t=4))
        nc.scalar.dma_start(out=gain_row[0:1, :], in_=rms2_scale.unsqueeze(0))
        nc.scalar.activation(out=warm[:, 1:2], in_=warm[:, 0:1], func=ACT.Abs_reciprocal_sqrt)
        make_identity(nc, ident[:])
        nc.gpsimd.memset(neghalf[:], -0.5)

        def load_scales(dst, src, lo, hi):
            for r in range(4):
                nc.sync.dma_start(
                    out=dst[r : P : 32, :, :].bitcast(I32),
                    in_=src[:, r : 16 : 4, lo:hi].rearrange("g q n -> q g n").bitcast(I32),
                )

        def load_words(dst, src, lo, hi):
            nc.sync.dma_start(out=dst[:], in_=src[:, :, 2 * lo : 2 * hi].rearrange("g p b -> p g b"))

        load_scales(wo_sc, w_o_scales, 0, D)
        load_words(wo, w_o_words, 0, D)
        nc.sync.dma_start(out=a_bytes[:, 1:3, :], in_=attn_bytes[1:3].rearrange("i p d -> p i d"))
        nc.sync.dma_start(out=x_sb[:, 0, :], in_=x[0])
        wg = {}
        wu = {}

        def load_chunks(lo, hi):
            tg = keep.tile([P, 2, 2 * (hi - lo)], U8, align_bytes=256, name="wg" + str(lo))
            tu = keep.tile([P, 2, 2 * (hi - lo)], U8, align_bytes=256, name="wu" + str(lo))
            load_words(tg, w_gate_words, lo, hi)
            load_words(tu, w_up_words, lo, hi)
            for c in range(lo // NC, hi // NC):
                wg[c] = (tg, 2 * (NC * c - lo))
                wu[c] = (tu, 2 * (NC * c - lo))

        load_scales(wg_sc[0], w_gate_scales, 0, SPLIT)
        load_scales(wu_sc[0], w_up_scales, 0, SPLIT)
        load_chunks(0, 512)
        load_chunks(512, 1024)
        nc.sync.dma_start(out=x_sb[:, 1, :], in_=x[1])
        load_chunks(1024, 2048)
        nc.sync.dma_start(out=a_bytes[:, 3, :], in_=attn_bytes[3])
        load_chunks(2048, 3072)

        def late_loads():
            load_scales(wg_sc[1], w_gate_scales, SPLIT, M)
            load_scales(wu_sc[1], w_up_scales, SPLIT, M)
            load_chunks(3072, 4096)
            nc.sync.dma_start(out=x_sb[:, 2, :], in_=x[2])
            nc.sync.dma_start(out=x_sb[:, 3, :], in_=x[3])

        abf = {}
        tbank = {}
        agrp = {}
        acod = {}
        asca = {}
        pbank = {}
        ss = {}
        rstd = {}
        hbf = {}
        hgrp = {}
        hcod = {}
        hsca = {}

        def cast(i, g, on_vector):
            if i not in abf:
                t = work.tile([P, D], BF16, align_bytes=256, name="abf")
                abf[i] = t
            o = abf[i][:, NC * g : NC * (g + 1)]
            s = a_bytes[:, i, NC * g : NC * (g + 1)].bitcast(F8)
            if on_vector:
                nc.vector.tensor_copy(out=o, in_=s)
            else:
                nc.scalar.copy(out=o, in_=s)

        def turn_attn(i, g, dst):
            words = abf[i][:].bitcast(F32)
            tbank[(i, g)] = dst
            for u in (0, 1):
                nc.tensor.transpose(dst[:, u, :], words[:, 256 * g + u : 256 * (g + 1) : 2], ident[:])

        def turn_attn_both(i, k):
            b = bank([P, 2, 2, P], k)
            turn_attn(i, 0, b[:, 0])
            turn_attn(i, 1, b[:, 1])

        def scale_attn(i, g):
            if i not in agrp:
                t = work.tile([P, 2, P, 2, 2], BF16, align_bytes=256, name="agrp")
                agrp[i] = t
            src = tbank[(i, g)].rearrange("p u r -> p (u r)").bitcast(BF16)
            src = src.rearrange("p (u r e) -> p r u e", u=2, e=2)
            sc = a_sc[:, g, :].rearrange("p (u e) -> p u e", u=2).unsqueeze(1).to_broadcast([P, P, 2, 2])
            nc.vector.tensor_tensor(out=agrp[i][:, g], in0=src, in1=sc, op=ALU.mult)

        def quant_attn(i, lo, hi):
            if i not in acod:
                t = work.tile([P, 2 * P], U32, align_bytes=256, name="acod")
                acod[i] = t
                t2 = work.tile([P, 2 * P], U8, align_bytes=256, name="asca")
                asca[i] = t2
            nc.vector.quantize_mx(
                out=acod[i][:, P * lo : P * hi].bitcast(FP8X4),
                scales=asca[i][:, P * lo : P * hi],
                in_=agrp[i][:, lo:hi].rearrange("p g r u e -> p (g r u e)"),
            )

        def mm1(i, banks):
            pbank[i] = banks
            for n in (0, 1):
                for g in (0, 1):
                    nc.tensor.matmul_mx(
                        out=pbank[i][n][:],
                        lhsT=acod[i][:, P * g : P * (g + 1)].bitcast(FP8X4),
                        lhsT_scale=asca[i][:, P * g : P * (g + 1)],
                        rhs=wo[:, g, 2 * NC * n : 2 * NC * (n + 1)].bitcast(FP4X4),
                        rhs_scale=wo_sc[:, g, NC * n : NC * (n + 1)],
                        start=(g == 0),
                        stop=(g == 1),
                    )

        def add_x(i, lo, hi):
            n = lo // NC
            nc.vector.tensor_tensor(
                out=xmid[i][:, lo:hi], in0=pbank[i][n][:, lo - NC * n : hi - NC * n], in1=x_sb[:, i, lo:hi], op=ALU.add)

        def square(i, k, lo, hi):
            if i not in ss:
                t = work.tile([P, 3], F32, align_bytes=256, name="ss")
                ss[i] = t
            nc.scalar.activation(
                out=sqj[:, : hi - lo], in_=xmid[i][:, lo:hi], func=ACT.Square, scale=1.0 / 32.0, accum_out=ss[i][:, k : k + 1])

        def root_two(i):
            ms = work.tile([P, 1], F32, align_bytes=256, name="ms")
            nc.gpsimd.tensor_scalar(out=ms[:], in0=ss[i][:, 0:1], scalar1=ss[i][:, 1:2], scalar2=EPS, op0=ALU.add, op1=ALU.add)
            return ms

        def root_end(i, ms):
            r = work.tile([P, 1], F32, align_bytes=256, name="rstd")
            nc.gpsimd.tensor_tensor(out=r[:], in0=ms[:], in1=neghalf[:], op=ALU.pow)
            rstd[i] = r

        def split_words(ap):
            return ap.rearrange("q (p u e) -> q u p e", u=2, e=2)

        def h_tile(i):
            if i not in hbf:
                t = work.tile([P, 2, 2, P, 2], BF16, align_bytes=256, name="hbf")
                hbf[i] = t

        ys = {}

        def gain_y(i, g, engine):
            if i not in ys:
                t = work.tile([P, 2, NC], F32, align_bytes=256, name="y", bufs=2)
                ys[i] = t
            cols = slice(NC * g, NC * (g + 1))
            engine.tensor_tensor(
                out=ys[i][:, g].rearrange("q (u p e) -> q u p e", u=2, e=2),
                in0=split_words(xmid[i][:, cols]), in1=split_words(gain[:, cols]), op=ALU.mult)

        def h_norm(i, lo, hi):
            h_tile(i)
            nc.vector.tensor_scalar(
                out=hbf[i][:, lo:hi].rearrange("q g u p e -> q (g u p e)"),
                in0=ys[i][:, lo:hi].rearrange("q g k -> q (g k)"), scalar1=rstd[i][:], scalar2=None, op0=ALU.mult)

        def turn_h(i, g, b):
            words = hbf[i][:].rearrange("q g u p e -> q (g u p e)").bitcast(F32)
            for u in (0, 1):
                nc.tensor.transpose(b[:, u, :], words[:, P * (2 * g + u) : P * (2 * g + u + 1)], ident[:])

        def copy_h(i, lo, hi, b, on_vector):
            if i not in hgrp:
                t = work.tile([P, 2, 4 * P], BF16, align_bytes=256, name="hgrp")
                hgrp[i] = t
            o = hgrp[i][:, lo:hi].bitcast(F32).rearrange("p g (r u) -> p g r u", u=2)
            s = b.rearrange("p g u r -> p g r u")
            if on_vector:
                nc.vector.tensor_copy(out=o, in_=s)
            else:
                nc.scalar.copy(out=o, in_=s)

        def quant_h(i, lo, hi):
            if i not in hcod:
                t = work.tile([P, 2 * P], U32, align_bytes=256, name="hcod")
                t2 = work.tile([P, 2 * P], U8, align_bytes=256, name="hsca")
                hcod[i], hsca[i] = t, t2
            nc.vector.quantize_mx(
                out=hcod[i][:, P * lo : P * hi].bitcast(FP8X4),
                scales=hsca[i][:, P * lo : P * hi],
                in_=hgrp[i][:, lo:hi].rearrange("p g w -> p (g w)"),
            )

        def mm2(i, c, w, w_sc, lo, width):
            b = next_bank([P, width])
            step = NC if width == NC else P
            half = int(NC * c >= SPLIT)
            first = NC * c - SPLIT * half
            for at_col in range(0, width, step):
              for g in (0, 1):
                nc.tensor.matmul_mx(
                    out=b[:, at_col : at_col + step],
                    lhsT=hcod[i][:, P * g : P * (g + 1)].bitcast(FP8X4),
                    lhsT_scale=hsca[i][:, P * g : P * (g + 1)],
                    rhs=w[c][0][:, g, w[c][1] + 2 * (lo + at_col) : w[c][1] + 2 * (lo + at_col + step)].bitcast(FP4X4),
                    rhs_scale=w_sc[half][:, g, first + lo + at_col : first + lo + at_col + step],
                    start=(g == 0),
                    stop=(g == 1),
                )
            return b

        def store_xmid(i):
            nc.sync.dma_start(out=out_0[i], in_=xmid[i][:])

        def dummies(k, b):
            t = bank([P, NC], b)
            for j in range(k):
                nc.tensor.matmul(t[:, :P], ones[:], ones[:], start=True, stop=True)

        dummies(22, 5)
        cast(0, 0, True)
        cast(0, 1, False)
        nc.gpsimd.tensor_copy(out=warm[:, 2:3], in_=abf[0][:, 0:1])
        for t in (wg_sc[1], wu_sc[1]):
            nc.gpsimd.memset(t[:].rearrange("p g n -> p (g n)").bitcast(I32), 0)
        turn_attn(0, 0, bank([P, 2, P], 0))
        turn_attn(0, 1, bank([P, 2, P], 1))
        gb = [bank([P, NC], 2), bank([P, NC], 3)]
        for n in (0, 1):
            nc.tensor.matmul(gb[n][:], ones[:], gain_row[:, NC * n : NC * (n + 1)], start=True, stop=True)
        for n in (0, 1):
            nc.scalar.copy(out=gain[:, NC * n : NC * (n + 1)], in_=gb[n][:])
        scale_attn(0, 0)
        scale_attn(0, 1)
        quant_attn(0, 0, 1)
        quant_attn(0, 1, 2)
        dummies(PL["d1"], 5)
        mm1(0, [bank([P, NC], 0), bank([P, NC], 1)])
        cast(1, 0, True)
        cast(1, 1, True)
        cast(2, 0, False)
        cast(2, 1, False)
        add_x(0, 0, 512)
        square(0, 0, 0, 512)
        add_x(0, 512, 768)
        square(0, 1, 512, 768)
        ms0 = root_two(0)
        add_x(0, 768, 1024)
        square(0, 2, 768, 1024)
        r0 = work.tile([P, 1], F32, align_bytes=256, name="rstd")
        nc.scalar.activation(out=r0[:], in_=ss[0][:, 2:3], func=ACT.Abs_reciprocal_sqrt, bias=ms0[:])
        rstd[0] = r0
        turn_attn_both(1, 4)
        turn_attn_both(2, 7)
        dummies(PL["d2"], 2)
        gain_y(0, 0, nc.vector)
        gain_y(0, 1, nc.vector)
        h_norm(0, 0, 1)
        h_norm(0, 1, 2)
        hb = [bank([P, 1, 2, P], 6), bank([P, 1, 2, P], 3)]
        turn_h(0, 0, hb[0][:, 0])
        turn_h(0, 1, hb[1][:, 0])
        scale_attn(1, 0)
        copy_h(0, 0, 1, hb[0], False)
        nc.scalar.activation(out=warm[:, 1:2], in_=warm[:, 0:1], func=ACT.Silu)
        copy_h(0, 1, 2, hb[1], True)
        quant_h(0, 0, 1)
        quant_h(0, 1, 2)
        dummies(PL["d3"], 2)
        scale_attn(1, 1)
        quant_attn(1, 0, 2)
        late_loads()

        def turn_and_copy_h(i, k):
            b = next_bank([P, 2, 2, P]) if k is None else bank([P, 2, 2, P], k)
            turn_h(i, 0, b[:, 0])
            turn_h(i, 1, b[:, 1])
            copy_h(i, 0, 2, b, False)

        at = {}

        def put(pos, *fs):
            at.setdefault(pos, []).extend(fs)

        def plan_rest(i, pos, k):
            put(pos, lambda: mm1(i, [next_bank([P, NC]), next_bank([P, NC])]), lambda: add_x(i, 0, 512))
            put(pos + 1, lambda: add_x(i, 512, 1024), lambda: square(i, 0, 0, 512), lambda: gain_y(i, 0, nc.gpsimd))
            put(pos + 2, lambda: square(i, 1, 512, 1024), lambda: gain_y(i, 1, nc.gpsimd), lambda: root_end(i, root_two(i)), lambda: store_xmid(i))
            put(pos + 4, lambda: h_norm(i, 0, 2))
            put(pos + 6, lambda: turn_and_copy_h(i, k), lambda: quant_h(i, 0, 2))

        put(PL["m1"], lambda: mm1(1, [next_bank([P, NC]), next_bank([P, NC])]), lambda: add_x(1, 0, 512), lambda: square(1, 0, 0, 512))
        put(PL["a1"], lambda: add_x(1, 512, 1024), lambda: square(1, 1, 512, 1024), lambda: root_end(1, root_two(1)))
        eng = nc.vector if PL["yv"] else nc.gpsimd
        put(PL["y0"], lambda: gain_y(1, 0, eng))
        put(PL["y1"], lambda: gain_y(1, 1, eng))
        put(PL["h"], lambda: h_norm(1, 0, 2))
        put(PL["t"], lambda: turn_and_copy_h(1, None), lambda: turn_attn_both(3, 6))
        put(PL["qh"], lambda: quant_h(1, 0, 2))
        put(PL["s2"], lambda: store_xmid(1), lambda: scale_attn(2, 0))
        put(PL["s2b"], lambda: scale_attn(2, 1), lambda: quant_attn(2, 0, 2))
        put(PL["c3"], lambda: cast(3, 0, False))
        put(PL["c3"] + 1, lambda: cast(3, 1, False))
        plan_rest(2, PL["r2"], 7)
        put(PL["s3"], lambda: scale_attn(3, 0))
        put(PL["s3"] + 1, lambda: scale_attn(3, 1), lambda: quant_attn(3, 0, 2))
        plan_rest(3, PL["r3"], 6)

        sequence = [(i, c) for i in (0, 1) for c in range(6)]
        sequence += [(i, c) for i in (0, 1) for c in range(6, CHUNKS)]
        sequence += [(i, c) for i in (2, 3) for c in range(CHUNKS)]
        for pos, (i, c) in enumerate(sequence):
                last = i == NT - 1 and c == CHUNKS - 1
                pieces = ((0, 256), (256, 128), (384, 128)) if last else ((0, NC),)
                for lo, width in pieces:
                    bg = mm2(i, c, wg, wg_sc, lo, width)
                    bu = mm2(i, c, wu, wu_sc, lo, width)
                    s = work.tile([P, NC], F32, align_bytes=256, name="s")
                    nc.scalar.activation(out=s[:, :width], in_=bg[:], func=ACT.Silu)
                    o = outp.tile([P, NC], F32, align_bytes=256, name="o")
                    nc.vector.tensor_tensor(out=o[:, :width], in0=bu[:], in1=s[:, :width], op=ALU.mult)
                    first = NC * c + lo
                    nc.sync.dma_start(out=out_1[i, :, first : first + width], in_=o[:, :width])
                if pos == PL["st0"]:
                    store_xmid(0)
                for step in at.get(pos, []):
                    step()
